import numpy as np
import ml_dtypes


def mxq(x, axis, fmt="e4m3"):
    dtype, down = {"e4m3": (ml_dtypes.float8_e4m3fn, 7), "e5m2": (ml_dtypes.float8_e5m2, 14)}[fmt]
    v = np.moveaxis(np.asarray(x, np.float32).astype(ml_dtypes.bfloat16).astype(np.float64), axis, -1)
    blocks = v.reshape(v.shape[:-1] + (-1, 32))
    amax = np.abs(blocks).max(-1, keepdims=True)
    byte = np.maximum(np.where(amax > 0, np.frexp(amax)[1] - 1 + 127, 0) - down, 1)
    scale = np.exp2(byte - 127.0)
    codes = (blocks / scale).astype(np.float32).astype(dtype).astype(np.float64)
    return np.moveaxis((codes * scale).reshape(v.shape), -1, axis)


WIDE = False


def mx_kscale(k):
    if not WIDE:
        return np.ones(k)
    levels = np.array([10, -10, 5, -5, 0])
    if k % 512:
        return np.exp2(np.random.permutation(np.resize(levels, k // 32))).repeat(32)
    a = np.empty((k // 512, 16))
    for p in range(k // 512):
        a[p, :8] = np.random.permutation(np.resize(levels, 8))
        for g in range(8):
            far = levels[np.abs(levels - a[p, g]) >= 10]
            a[p, g + 8] = far[np.random.randint(len(far))]
    return np.exp2(a.ravel()).repeat(32)


BF16 = ml_dtypes.bfloat16


def bf(x):
    return np.asarray(x, np.float32).astype(BF16)


def f64(x):
    return np.asarray(x).astype(np.float64)


N, K, F, NB = 1024, 512, 384, 32


def setup_inputs():
    s = mx_kscale(N)
    c = s / s.min()
    r = s.max() / s
    edge = np.random.random_sample((N, N)) < NB / N
    return {"h_ln": bf(np.random.standard_normal((N, F)) * r[:, None]),
            "adj": bf(np.random.random_sample((N, N)) * edge * c[None, :]),
            "W2": bf(np.random.standard_normal((F, F)) * 2.0 / np.sqrt(F)),
            "b2": bf(np.random.standard_normal(F) * 0.2)}


def reference(h_ln, adj, W2, b2):
    a = f64(adj)
    h = f64(h_ln) @ f64(W2) + f64(b2)
    deg = a.sum(axis=1) + 1.0
    dinv = np.where(deg > 0, deg ** -0.5, 0.0)
    hs = dinv[:, None] * h
    agg = (mxq(a, 1, "e4m3") @ mxq(hs, 0, "e4m3")) + hs
    return dinv[:, None] * agg

@@ -1,0 +1,271 @@
+import concourse.mybir as mybir
+from concourse.masks import make_identity
+
+F32 = mybir.dt.float32
+BF16 = mybir.dt.bfloat16
+I32 = mybir.dt.int32
+U32 = mybir.dt.uint32
+U8 = mybir.dt.uint8
+FP8X4 = mybir.dt.float8_e4m3fn_x4
+ALU = mybir.AluOpType
+ACT = mybir.ActivationFunctionType
+
+P = 128
+NODES = 1024
+FEAT = 384
+K_BLOCKS = FEAT // P
+PAIR = 2
+CHUNKS = NODES // (P * PAIR)
+TILES = CHUNKS * PAIR
+PACK = 4
+PASSES = NODES // (P * PACK)
+HALVES = PACK // PAIR
+MX_COLS = 512
+FEAT_PARTS = ((0, 256), (256, 128))
+BANKS = 8
+
+FLOPS = 2 * NODES * FEAT * FEAT + 2 * NODES * NODES * FEAT
+
+
+def tile_gcnlayer_pb_kernel(tc, h_ln, adj, W2, b2, out):
+    nc = tc.nc
+
+    h_rows = h_ln.rearrange("(g p u e) k -> p g u e k", p=P, u=HALVES, e=PAIR)
+    adj_rows = adj.rearrange("(g p u e) j -> p g u e j", p=P, u=HALVES, e=PAIR)
+    out_rows = out.rearrange("(g p u e) f -> p g u e f", p=P, u=HALVES, e=PAIR)
+
+    with (
+        tc.tile_pool(name="keep", bufs=1) as keep,
+        tc.psum_pool(name="psum", bufs=BANKS) as psum,
+    ):
+        h_sb = keep.tile([P, CHUNKS, PAIR, FEAT], BF16)
+        w_sb = keep.tile([P, K_BLOCKS, FEAT], BF16)
+        adj_sb = keep.tile([P, CHUNKS, PAIR, NODES], BF16)
+        bias_rows = keep.tile([P, FEAT], BF16)
+        ones_bf = keep.tile([P, P], BF16)
+        bias_sb = keep.tile([P, FEAT], F32)
+        ident_bf = keep.tile([P, P], BF16)
+        ident_f32 = keep.tile([P, P], F32)
+        one = keep.tile([P, 1], F32)
+        warm = keep.tile([P, 1], F32)
+        hT_sb = keep.tile([P, CHUNKS, PAIR, K_BLOCKS, P], BF16)
+        hb = keep.tile([P, TILES, FEAT], F32)
+        hs_self = keep.tile([P, TILES, FEAT], F32)
+        row_sums = keep.tile([P, PASSES, 8], F32)
+        sum_scratch = keep.tile([P, TILES, NODES], BF16)
+        root = keep.tile([P, TILES], F32)
+        dinv = keep.tile([P, TILES], F32)
+        dinv_sq = keep.tile([P, TILES], F32)
+        adj_grouped = keep.tile([P, TILES, PASSES, P, PACK], BF16, align_bytes=64)
+        adj_codes = keep.tile([P, TILES, PASSES, P], U32, align_bytes=64)
+        adj_scales = keep.tile([P, TILES, PASSES, P], U8, align_bytes=64)
+        hs_grouped = keep.tile([P, PASSES, FEAT, PACK], BF16, align_bytes=64)
+        hs_codes = keep.tile([P, PASSES, MX_COLS], U32, align_bytes=64)
+        hs_scales = keep.tile([P, PASSES, MX_COLS], U8, align_bytes=64)
+        out_sb = keep.tile([P, TILES, FEAT], F32)
+
+        adj_words = adj_sb[:].bitcast(F32)
+        adj_grouped_words = adj_grouped[:].bitcast(F32)
+        agg_banks = {}
+
+        def load_adj(a):
+            g, u = divmod(a, HALVES)
+            nc.sync.dma_start(out=adj_sb[:, a], in_=adj_rows[:, g, u])
+
+        def load_h(g):
+            two = slice(g * HALVES, (g + 1) * HALVES)
+            nc.sync.dma_start(out=h_sb[:, two], in_=h_rows[:, g])
+
+        def spread_bias():
+            bias_ps = psum.tile([P, FEAT], F32, tag="bank")
+            nc.tensor.matmul(bias_ps[:], lhsT=ones_bf[:], rhs=bias_rows[:], start=True, stop=True)
+            nc.scalar.copy(out=bias_sb[:], in_=bias_ps[:])
+
+        def row_sum(n):
+            g, t = divmod(n, PACK)
+            rows = adj_sb[:, n // PAIR, n % PAIR, :]
+            if g == 0:
+                nc.vector.scalar_tensor_tensor(
+                    out=sum_scratch[:, n, :].bitcast(F32),
+                    in0=rows[:, 0 : NODES // 2],
+                    scalar=1.0,
+                    in1=rows[:, NODES // 2 : NODES],
+                    op0=ALU.mult,
+                    op1=ALU.add,
+                    accum_out=row_sums[:, g, t : t + 1],
+                )
+            else:
+                nc.scalar.activation(
+                    out=sum_scratch[:, n, :],
+                    in_=rows,
+                    func=ACT.Copy,
+                    accum_out=row_sums[:, g, t : t + 1],
+                )
+
+        def root_of_degree(g):
+            four = slice(g * PACK, (g + 1) * PACK)
+            nc.scalar.activation(
+                out=root[:, four], in_=row_sums[:, g, 0:PACK], func=ACT.Sqrt, bias=1.0
+            )
+
+        def transpose_adj(n):
+            adjT_ps = psum.tile([P, PASSES * HALVES, P], F32, tag="bank")
+            for b in range(PASSES * HALVES):
+                g, u = divmod(b, HALVES)
+                first = g * P * HALVES + u
+                nc.tensor.transpose(
+                    adjT_ps[:, b, :],
+                    adj_words[:, n // PAIR, n % PAIR, first : (g + 1) * P * HALVES : HALVES],
+                    ident_f32[:],
+                )
+            nc.scalar.copy(
+                out=adj_grouped_words[:, n],
+                in_=adjT_ps[:].rearrange("p (g u) i -> p g i u", u=HALVES),
+            )
+
+        def quantise_adj(a):
+            pair = slice(a * PAIR, (a + 1) * PAIR)
+            nc.vector.quantize_mx(
+                out=adj_codes[:, pair].rearrange("p n g i -> p (n g i)").bitcast(FP8X4),
+                scales=adj_scales[:, pair].rearrange("p n g i -> p (n g i)"),
+                in_=adj_grouped[:, pair].rearrange("p n g i t -> p (n g i t)"),
+            )
+
+        def transpose_h(a):
+            hT_ps = psum.tile([P, PAIR, K_BLOCKS, P], BF16, tag="bank")
+            for e in range(PAIR):
+                for kb in range(K_BLOCKS):
+                    nc.tensor.transpose(
+                        hT_ps[:, e, kb, :], h_sb[:, a, e, kb * P : (kb + 1) * P], ident_bf[:]
+                    )
+            nc.scalar.copy(out=hT_sb[:, a], in_=hT_ps[:])
+
+        def linear(n):
+            h_ps = psum.tile([P, FEAT], F32, tag="bank")
+            for kb in range(K_BLOCKS):
+                nc.tensor.matmul(
+                    h_ps[:],
+                    lhsT=hT_sb[:, n // PAIR, n % PAIR, kb, :],
+                    rhs=w_sb[:, kb, :],
+                    start=(kb == 0),
+                    stop=(kb == K_BLOCKS - 1),
+                )
+            nc.vector.tensor_tensor(out=hb[:, n, :], in0=h_ps[:], in1=bias_sb[:], op=ALU.add)
+
+        def quantise_hs(g):
+            four = slice(g * PACK, (g + 1) * PACK)
+            nc.vector.reciprocal(out=dinv[:, four], in_=root[:, four])
+            for f0, width in FEAT_PARTS:
+                nc.vector.tensor_tensor(
+                    out=hs_grouped[:, g, f0 : f0 + width, :],
+                    in0=hb[:, four, f0 : f0 + width].rearrange("p t f -> p f t"),
+                    in1=dinv[:, four].unsqueeze(1).to_broadcast([P, width, PACK]),
+                    op=ALU.mult,
+                )
+            for f0, width in FEAT_PARTS:
+                nc.vector.quantize_mx(
+                    out=hs_codes[:, g, f0 : f0 + width].bitcast(FP8X4),
+                    scales=hs_scales[:, g, f0 : f0 + width],
+                    in_=hs_grouped[:, g, f0 : f0 + width, :].rearrange("p f t -> p (f t)"),
+                )
+
+        def self_terms(g):
+            four = slice(g * PACK, (g + 1) * PACK)
+            nc.scalar.square(out=dinv_sq[:, four], in_=dinv[:, four])
+            for n in range(g * PACK, (g + 1) * PACK):
+                nc.scalar.activation(
+                    out=hs_self[:, n, :],
+                    in_=hb[:, n, :],
+                    func=ACT.Copy,
+                    scale=dinv_sq[:, n : n + 1],
+                )
+
+        def aggregate(n, g):
+            if g == 0:
+                agg_banks[n] = psum.tile([P, MX_COLS], F32, tag="bank", name="agg_ps")
+            nc.tensor.matmul_mx(
+                out=agg_banks[n][:],
+                lhsT=adj_codes[:, n, g, :].bitcast(FP8X4),
+                lhsT_scale=adj_scales[:, n, g, :],
+                rhs=hs_codes[:, g, :].bitcast(FP8X4),
+                rhs_scale=hs_scales[:, g, :],
+                start=(g == 0),
+                stop=(g == PASSES - 1),
+            )
+
+        def finish(n):
+            nc.vector.scalar_tensor_tensor(
+                out=out_sb[:, n, :],
+                in0=agg_banks[n][:, 0:FEAT],
+                scalar=dinv[:, n : n + 1],
+                in1=hs_self[:, n, :],
+                op0=ALU.mult,
+                op1=ALU.add,
+            )
+            g, t = divmod(n, PACK)
+            nc.sync.dma_start(out=out_rows[:, g, t // PAIR, t % PAIR, :], in_=out_sb[:, n, :])
+
+        with tc.manual_schedule():
+            nc.gpsimd.memset(bias_rows[:], 0.0)
+            nc.gpsimd.memset(ones_bf[:], 1.0)
+            load_adj(0)
+            nc.sync.dma_start(out=bias_rows[0:1, :], in_=b2.unsqueeze(0))
+            load_h(0)
+            load_adj(1)
+            nc.sync.dma_start(out=w_sb[:], in_=W2.rearrange("(kb p) f -> p kb f", p=P))
+            load_adj(2)
+            load_adj(3)
+            load_h(1)
+            make_identity(nc, ident_f32[:])
+            make_identity(nc, ident_bf[:])
+            nc.vector.memset(one[:], 1.0)
+            nc.scalar.sqrt(out=warm[:], in_=one[:])
+            nc.vector.memset(hs_codes[:, :, FEAT:MX_COLS].bitcast(I32), 0)
+            nc.vector.memset(hs_scales[:, :, FEAT:MX_COLS].bitcast(I32), 0)
+
+            row_sum(0)
+            row_sum(1)
+            row_sum(2)
+            transpose_adj(0)
+            transpose_adj(1)
+            quantise_adj(0)
+            row_sum(3)
+            transpose_h(0)
+            transpose_h(1)
+            spread_bias()
+            transpose_adj(2)
+            transpose_adj(3)
+            root_of_degree(0)
+            linear(0)
+            linear(1)
+            quantise_adj(1)
+            linear(2)
+            linear(3)
+            quantise_hs(0)
+
+            row_sum(4)
+            row_sum(5)
+            transpose_h(2)
+            transpose_h(3)
+            row_sum(6)
+            row_sum(7)
+            root_of_degree(1)
+            for n in range(PACK, TILES):
+                transpose_adj(n)
+            for n in range(PACK, TILES):
+                linear(n)
+            quantise_hs(1)
+            quantise_adj(2)
+            quantise_adj(3)
+            for g in range(PASSES):
+                self_terms(g)
+
+            for n in range(PACK):
+                aggregate(n, 0)
+            for n in range(PACK):
+                aggregate(n, 1)
+                finish(n)
+            for n in range(PACK, TILES):
+                aggregate(n, 0)
+                aggregate(n, 1)
+                finish(n)

@@ -22,6 +22,7 @@ PASSES = NODES // (P * PACK)
 HALVES = PACK // PAIR
 MX_COLS = 512
 FEAT_PARTS = ((0, 256), (256, 128))
+RUN = 4
 BANKS = 8
 
 FLOPS = 2 * NODES * FEAT * FEAT + 2 * NODES * NODES * FEAT
@@ -157,9 +158,14 @@ def tile_gcnlayer_pb_kernel(tc, h_ln, adj, W2, b2, out):
             nc.vector.reciprocal(out=dinv[:, four], in_=root[:, four])
             for f0, width in FEAT_PARTS:
                 nc.vector.tensor_tensor(
-                    out=hs_grouped[:, g, f0 : f0 + width, :],
-                    in0=hb[:, four, f0 : f0 + width].rearrange("p t f -> p f t"),
-                    in1=dinv[:, four].unsqueeze(1).to_broadcast([P, width, PACK]),
+                    out=hs_grouped[:, g, f0 : f0 + width, :].rearrange(
+                        "p (c i) t -> p c t i", i=RUN
+                    ),
+                    in0=hb[:, four, f0 : f0 + width].rearrange("p t (c i) -> p c t i", i=RUN),
+                    in1=dinv[:, four]
+                    .unsqueeze(1)
+                    .unsqueeze(3)
+                    .to_broadcast([P, width // RUN, PACK, RUN]),
                     op=ALU.mult,
                 )
             for f0, width in FEAT_PARTS:

@@ -14,14 +14,13 @@ P = 128
 NODES = 1024
 FEAT = 384
 K_BLOCKS = FEAT // P
-PAIR = 2
-CHUNKS = NODES // (P * PAIR)
-TILES = CHUNKS * PAIR
 PACK = 4
 PASSES = NODES // (P * PACK)
+TILES = PASSES * PACK
+PAIR = 2
 HALVES = PACK // PAIR
-MX_COLS = 512
 FEAT_PARTS = ((0, 256), (256, 128))
+MX_COLS = 512
 RUN = 4
 BANKS = 8
 
@@ -31,17 +30,17 @@ FLOPS = 2 * NODES * FEAT * FEAT + 2 * NODES * NODES * FEAT
 def tile_gcnlayer_pb_kernel(tc, h_ln, adj, W2, b2, out):
     nc = tc.nc
 
-    h_rows = h_ln.rearrange("(g p u e) k -> p g u e k", p=P, u=HALVES, e=PAIR)
-    adj_rows = adj.rearrange("(g p u e) j -> p g u e j", p=P, u=HALVES, e=PAIR)
-    out_rows = out.rearrange("(g p u e) f -> p g u e f", p=P, u=HALVES, e=PAIR)
+    h_rows = h_ln.rearrange("(g p t) k -> p g t k", p=P, t=PACK)
+    adj_rows = adj.rearrange("(g p t) j -> p g t j", p=P, t=PACK)
+    out_rows = out.rearrange("(g p t) f -> p g t f", p=P, t=PACK)
 
     with (
         tc.tile_pool(name="keep", bufs=1) as keep,
         tc.psum_pool(name="psum", bufs=BANKS) as psum,
     ):
-        h_sb = keep.tile([P, CHUNKS, PAIR, FEAT], BF16)
+        h_sb = keep.tile([P, TILES, FEAT], BF16)
         w_sb = keep.tile([P, K_BLOCKS, FEAT], BF16)
-        adj_sb = keep.tile([P, CHUNKS, PAIR, NODES], BF16)
+        adj_sb = keep.tile([P, TILES, NODES], BF16)
         bias_rows = keep.tile([P, FEAT], BF16)
         ones_bf = keep.tile([P, P], BF16)
         bias_sb = keep.tile([P, FEAT], F32)
@@ -49,7 +48,7 @@ def tile_gcnlayer_pb_kernel(tc, h_ln, adj, W2, b2, out):
         ident_f32 = keep.tile([P, P], F32)
         one = keep.tile([P, 1], F32)
         warm = keep.tile([P, 1], F32)
-        hT_sb = keep.tile([P, CHUNKS, PAIR, K_BLOCKS, P], BF16)
+        hT_sb = keep.tile([P, TILES, K_BLOCKS, P], BF16)
         hb = keep.tile([P, TILES, FEAT], F32)
         hs_self = keep.tile([P, TILES, FEAT], F32)
         row_sums = keep.tile([P, PASSES, 8], F32)
@@ -66,128 +65,162 @@ def tile_gcnlayer_pb_kernel(tc, h_ln, adj, W2, b2, out):
         out_sb = keep.tile([P, TILES, FEAT], F32)
 
         adj_words = adj_sb[:].bitcast(F32)
+
         adj_grouped_words = adj_grouped[:].bitcast(F32)
+
         agg_banks = {}
 
-        def load_adj(a):
-            g, u = divmod(a, HALVES)
-            nc.sync.dma_start(out=adj_sb[:, a], in_=adj_rows[:, g, u])
+        def load_adj(n, count=1):
+            g, t = divmod(n, PACK)
+            nc.sync.dma_start(out=adj_sb[:, n : n + count, :], in_=adj_rows[:, g, t : t + count, :])
 
-        def load_h(g):
-            two = slice(g * HALVES, (g + 1) * HALVES)
-            nc.sync.dma_start(out=h_sb[:, two], in_=h_rows[:, g])
+        def load_h(n, count=PACK):
+            g, t = divmod(n, PACK)
+            nc.sync.dma_start(out=h_sb[:, n : n + count, :], in_=h_rows[:, g, t : t + count, :])
 
         def spread_bias():
             bias_ps = psum.tile([P, FEAT], F32, tag="bank")
             nc.tensor.matmul(bias_ps[:], lhsT=ones_bf[:], rhs=bias_rows[:], start=True, stop=True)
             nc.scalar.copy(out=bias_sb[:], in_=bias_ps[:])
 
-        def row_sum(n):
+        def sum_v(n):
             g, t = divmod(n, PACK)
-            rows = adj_sb[:, n // PAIR, n % PAIR, :]
-            if g == 0:
-                nc.vector.scalar_tensor_tensor(
-                    out=sum_scratch[:, n, :].bitcast(F32),
-                    in0=rows[:, 0 : NODES // 2],
-                    scalar=1.0,
-                    in1=rows[:, NODES // 2 : NODES],
-                    op0=ALU.mult,
-                    op1=ALU.add,
-                    accum_out=row_sums[:, g, t : t + 1],
-                )
-            else:
-                nc.scalar.activation(
-                    out=sum_scratch[:, n, :],
-                    in_=rows,
-                    func=ACT.Copy,
-                    accum_out=row_sums[:, g, t : t + 1],
-                )
+            nc.vector.scalar_tensor_tensor(
+                out=sum_scratch[:, n, :].bitcast(F32),
+                in0=adj_sb[:, n, 0 : NODES // 2],
+                scalar=1.0,
+                in1=adj_sb[:, n, NODES // 2 : NODES],
+                op0=ALU.mult,
+                op1=ALU.add,
+                accum_out=row_sums[:, g, t : t + 1],
+            )
 
-        def root_of_degree(g):
+        def sum_s(n):
+            g, t = divmod(n, PACK)
+            nc.scalar.activation(
+                out=sum_scratch[:, n, :],
+                in_=adj_sb[:, n, :],
+                func=ACT.Copy,
+                accum_out=row_sums[:, g, t : t + 1],
+            )
+
+        def dinv_of(g):
             four = slice(g * PACK, (g + 1) * PACK)
             nc.scalar.activation(
                 out=root[:, four], in_=row_sums[:, g, 0:PACK], func=ACT.Sqrt, bias=1.0
             )
 
-        def transpose_adj(n):
-            adjT_ps = psum.tile([P, PASSES * HALVES, P], F32, tag="bank")
+        def recip(g):
+            four = slice(g * PACK, (g + 1) * PACK)
+            nc.vector.reciprocal(out=dinv[:, four], in_=root[:, four])
+
+        adjT = {}
+
+        def tr_adj(n):
+            adjT_ps = psum.tile([P, PASSES * HALVES, P], F32, tag="bank", name="adjT_ps")
+            adjT[n] = adjT_ps
             for b in range(PASSES * HALVES):
                 g, u = divmod(b, HALVES)
                 first = g * P * HALVES + u
                 nc.tensor.transpose(
                     adjT_ps[:, b, :],
-                    adj_words[:, n // PAIR, n % PAIR, first : (g + 1) * P * HALVES : HALVES],
+                    adj_words[:, n, first : (g + 1) * P * HALVES : HALVES],
                     ident_f32[:],
                 )
-            nc.scalar.copy(
-                out=adj_grouped_words[:, n],
-                in_=adjT_ps[:].rearrange("p (g u) i -> p g i u", u=HALVES),
-            )
 
-        def quantise_adj(a):
-            pair = slice(a * PAIR, (a + 1) * PAIR)
+        def exit_adj(n, on_vector=False):
+            src = adjT[n][:].rearrange("p (g u) i -> p g i u", u=HALVES)
+            if on_vector:
+                nc.vector.tensor_copy(out=adj_grouped_words[:, n], in_=src)
+            else:
+                nc.scalar.copy(out=adj_grouped_words[:, n], in_=src)
+
+        def adj_T(n):
+            tr_adj(n)
+            exit_adj(n)
+
+        def q_adj(n, count=1):
+            tiles = slice(n, n + count)
             nc.vector.quantize_mx(
-                out=adj_codes[:, pair].rearrange("p n g i -> p (n g i)").bitcast(FP8X4),
-                scales=adj_scales[:, pair].rearrange("p n g i -> p (n g i)"),
-                in_=adj_grouped[:, pair].rearrange("p n g i t -> p (n g i t)"),
+                out=adj_codes[:, tiles].rearrange("p n g i -> p (n g i)").bitcast(FP8X4),
+                scales=adj_scales[:, tiles].rearrange("p n g i -> p (n g i)"),
+                in_=adj_grouped[:, tiles].rearrange("p n g i t -> p (n g i t)"),
             )
 
-        def transpose_h(a):
+        def tr_h(n):
             hT_ps = psum.tile([P, PAIR, K_BLOCKS, P], BF16, tag="bank")
             for e in range(PAIR):
                 for kb in range(K_BLOCKS):
                     nc.tensor.transpose(
-                        hT_ps[:, e, kb, :], h_sb[:, a, e, kb * P : (kb + 1) * P], ident_bf[:]
+                        hT_ps[:, e, kb, :], h_sb[:, n + e, kb * P : (kb + 1) * P], ident_bf[:]
                     )
-            nc.scalar.copy(out=hT_sb[:, a], in_=hT_ps[:])
+            nc.scalar.copy(out=hT_sb[:, n : n + PAIR], in_=hT_ps[:])
+
+        h_banks = {}
 
         def linear(n):
-            h_ps = psum.tile([P, FEAT], F32, tag="bank")
+            h_ps = psum.tile([P, FEAT], F32, tag="bank", name="h_ps")
+            h_banks[n] = h_ps
             for kb in range(K_BLOCKS):
                 nc.tensor.matmul(
                     h_ps[:],
-                    lhsT=hT_sb[:, n // PAIR, n % PAIR, kb, :],
+                    lhsT=hT_sb[:, n, kb, :],
                     rhs=w_sb[:, kb, :],
                     start=(kb == 0),
                     stop=(kb == K_BLOCKS - 1),
                 )
-            nc.vector.tensor_tensor(out=hb[:, n, :], in0=h_ps[:], in1=bias_sb[:], op=ALU.add)
 
-        def quantise_hs(g):
+        def linear_b(n):
+            h_ps = psum.tile([P, FEAT], F32, tag="bank", name="h_ps")
+            h_banks[n] = h_ps
+            nc.tensor.matmul(h_ps[:], lhsT=ones_bf[:], rhs=bias_rows[:], start=True, stop=False)
+            for kb in range(K_BLOCKS):
+                nc.tensor.matmul(
+                    h_ps[:],
+                    lhsT=hT_sb[:, n, kb, :],
+                    rhs=w_sb[:, kb, :],
+                    start=False,
+                    stop=(kb == K_BLOCKS - 1),
+                )
+
+        def exit_h(n):
+            nc.scalar.copy(out=hb[:, n, :], in_=h_banks[n][:])
+
+        def bias(n):
+            nc.vector.tensor_tensor(out=hb[:, n, :], in0=h_banks[n][:], in1=bias_sb[:], op=ALU.add)
+
+        def hs(g, part):
             four = slice(g * PACK, (g + 1) * PACK)
-            nc.vector.reciprocal(out=dinv[:, four], in_=root[:, four])
-            for f0, width in FEAT_PARTS:
-                nc.vector.tensor_tensor(
-                    out=hs_grouped[:, g, f0 : f0 + width, :].rearrange(
-                        "p (c i) t -> p c t i", i=RUN
-                    ),
-                    in0=hb[:, four, f0 : f0 + width].rearrange("p t (c i) -> p c t i", i=RUN),
-                    in1=dinv[:, four]
-                    .unsqueeze(1)
-                    .unsqueeze(3)
-                    .to_broadcast([P, width // RUN, PACK, RUN]),
-                    op=ALU.mult,
-                )
-            for f0, width in FEAT_PARTS:
-                nc.vector.quantize_mx(
-                    out=hs_codes[:, g, f0 : f0 + width].bitcast(FP8X4),
-                    scales=hs_scales[:, g, f0 : f0 + width],
-                    in_=hs_grouped[:, g, f0 : f0 + width, :].rearrange("p f t -> p (f t)"),
-                )
+            f0, width = FEAT_PARTS[part]
+            nc.vector.tensor_tensor(
+                out=hs_grouped[:, g, f0 : f0 + width, :].rearrange("p (c i) t -> p c t i", i=RUN),
+                in0=hb[:, four, f0 : f0 + width].rearrange("p t (c i) -> p c t i", i=RUN),
+                in1=dinv[:, four]
+                .unsqueeze(1)
+                .unsqueeze(3)
+                .to_broadcast([P, width // RUN, PACK, RUN]),
+                op=ALU.mult,
+            )
 
-        def self_terms(g):
+        def q_hs(g, part):
+            f0, width = FEAT_PARTS[part]
+            nc.vector.quantize_mx(
+                out=hs_codes[:, g, f0 : f0 + width].bitcast(FP8X4),
+                scales=hs_scales[:, g, f0 : f0 + width],
+                in_=hs_grouped[:, g, f0 : f0 + width, :].rearrange("p f t -> p (f t)"),
+            )
+
+        def sq(g):
             four = slice(g * PACK, (g + 1) * PACK)
             nc.scalar.square(out=dinv_sq[:, four], in_=dinv[:, four])
-            for n in range(g * PACK, (g + 1) * PACK):
-                nc.scalar.activation(
-                    out=hs_self[:, n, :],
-                    in_=hb[:, n, :],
-                    func=ACT.Copy,
-                    scale=dinv_sq[:, n : n + 1],
-                )
 
-        def aggregate(n, g):
-            if g == 0:
+        def self_s(n):
+            nc.scalar.activation(
+                out=hs_self[:, n, :], in_=hb[:, n, :], func=ACT.Copy, scale=dinv_sq[:, n : n + 1]
+            )
+
+        def mx(n, g, first=None, last=None):
+            if n not in agg_banks:
                 agg_banks[n] = psum.tile([P, MX_COLS], F32, tag="bank", name="agg_ps")
             nc.tensor.matmul_mx(
                 out=agg_banks[n][:],
@@ -208,20 +241,13 @@ def tile_gcnlayer_pb_kernel(tc, h_ln, adj, W2, b2, out):
                 op0=ALU.mult,
                 op1=ALU.add,
             )
-            g, t = divmod(n, PACK)
-            nc.sync.dma_start(out=out_rows[:, g, t // PAIR, t % PAIR, :], in_=out_sb[:, n, :])
+            store(n)
 
-        with tc.manual_schedule():
-            nc.gpsimd.memset(bias_rows[:], 0.0)
-            nc.gpsimd.memset(ones_bf[:], 1.0)
-            load_adj(0)
-            nc.sync.dma_start(out=bias_rows[0:1, :], in_=b2.unsqueeze(0))
-            load_h(0)
-            load_adj(1)
-            nc.sync.dma_start(out=w_sb[:], in_=W2.rearrange("(kb p) f -> p kb f", p=P))
-            load_adj(2)
-            load_adj(3)
-            load_h(1)
+        def store(n):
+            g, t = divmod(n, PACK)
+            nc.sync.dma_start(out=out_rows[:, g, t, :], in_=out_sb[:, n, :])
+
+        def consts():
             make_identity(nc, ident_f32[:])
             make_identity(nc, ident_bf[:])
             nc.vector.memset(one[:], 1.0)
@@ -229,49 +255,82 @@ def tile_gcnlayer_pb_kernel(tc, h_ln, adj, W2, b2, out):
             nc.vector.memset(hs_codes[:, :, FEAT:MX_COLS].bitcast(I32), 0)
             nc.vector.memset(hs_scales[:, :, FEAT:MX_COLS].bitcast(I32), 0)
 
-            row_sum(0)
-            row_sum(1)
-            row_sum(2)
-            transpose_adj(0)
-            transpose_adj(1)
-            quantise_adj(0)
-            row_sum(3)
-            transpose_h(0)
-            transpose_h(1)
+        with tc.manual_schedule():
+            nc.gpsimd.memset(bias_rows[:], 0.0)
+            nc.gpsimd.memset(ones_bf[:], 1.0)
+            load_adj(0,2)
+            nc.sync.dma_start(out=bias_rows[0:1, :], in_=b2.unsqueeze(0))
+            load_h(0)
+            load_adj(2,2)
+            nc.sync.dma_start(out=w_sb[:], in_=W2.rearrange("(kb p) f -> p kb f", p=P))
+            load_adj(4,2)
+            load_h(4)
+            load_adj(6,2)
+            consts()
+
+            sum_v(0)
+            sum_v(1)
+            adj_T(0)
+            adj_T(1)
+            tr_h(0)
+            tr_h(2)
             spread_bias()
-            transpose_adj(2)
-            transpose_adj(3)
-            root_of_degree(0)
+            sum_v(2)
+            q_adj(0,2)
+            sum_v(3)
+            adj_T(2)
+            adj_T(3)
+            dinv_of(0)
             linear(0)
+            bias(0)
             linear(1)
-            quantise_adj(1)
+            bias(1)
+            q_adj(2,2)
             linear(2)
+            bias(2)
             linear(3)
-            quantise_hs(0)
-
-            row_sum(4)
-            row_sum(5)
-            transpose_h(2)
-            transpose_h(3)
-            row_sum(6)
-            row_sum(7)
-            root_of_degree(1)
-            for n in range(PACK, TILES):
-                transpose_adj(n)
-            for n in range(PACK, TILES):
-                linear(n)
-            quantise_hs(1)
-            quantise_adj(2)
-            quantise_adj(3)
-            for g in range(PASSES):
-                self_terms(g)
-
-            for n in range(PACK):
-                aggregate(n, 0)
-            for n in range(PACK):
-                aggregate(n, 1)
+            bias(3)
+            recip(0)
+            hs(0,0)
+            hs(0,1)
+            sum_v(6)
+            sum_v(7)
+            q_hs(0,0)
+            q_hs(0,1)
+            sum_s(4)
+            sum_s(5)
+            tr_h(4)
+            tr_h(6)
+            sq(0)
+            for n in range(4,8):
+                linear_b(n)
+            self_s(0)
+            exit_h(4)
+            self_s(1)
+            exit_h(5)
+            self_s(2)
+            exit_h(6)
+            dinv_of(1)
+            self_s(3)
+            exit_h(7)
+            for n in range(4,8):
+                adj_T(n)
+            recip(1)
+            hs(1,0)
+            hs(1,1)
+            q_hs(1,0)
+            q_hs(1,1)
+            q_adj(4,2)
+            q_adj(6,2)
+            sq(1)
+            for n in range(4,8):
+                self_s(n)
+            for n in range(4):
+                mx(n,0)
+            for n in range(4):
+                mx(n,1)
                 finish(n)
-            for n in range(PACK, TILES):
-                aggregate(n, 0)
-                aggregate(n, 1)
+            for n in range(4,8):
+                mx(n,0)
+                mx(n,1)
                 finish(n)

@@ -53,7 +53,6 @@ def tile_gcnlayer_pb_kernel(tc, h_ln, adj, W2, b2, out):
         hs_self = keep.tile([P, TILES, FEAT], F32)
         row_sums = keep.tile([P, PASSES, 8], F32)
         sum_scratch = keep.tile([P, TILES, NODES], BF16)
-        root = keep.tile([P, TILES], F32)
         dinv = keep.tile([P, TILES], F32)
         dinv_sq = keep.tile([P, TILES], F32)
         adj_grouped = keep.tile([P, TILES, PASSES, P, PACK], BF16, align_bytes=64)
@@ -107,12 +106,11 @@ def tile_gcnlayer_pb_kernel(tc, h_ln, adj, W2, b2, out):
         def dinv_of(g):
             four = slice(g * PACK, (g + 1) * PACK)
             nc.scalar.activation(
-                out=root[:, four], in_=row_sums[:, g, 0:PACK], func=ACT.Sqrt, bias=1.0
+                out=dinv[:, four],
+                in_=row_sums[:, g, 0:PACK],
+                func=ACT.Abs_reciprocal_sqrt,
+                bias=1.0,
             )
-
-        def recip(g):
-            four = slice(g * PACK, (g + 1) * PACK)
-            nc.vector.reciprocal(out=dinv[:, four], in_=root[:, four])
 
         adjT = {}
 
@@ -170,13 +168,15 @@ def tile_gcnlayer_pb_kernel(tc, h_ln, adj, W2, b2, out):
                     stop=(kb == K_BLOCKS - 1),
                 )
 
-        def linear_b(n):
-            h_ps = psum.tile([P, FEAT], F32, tag="bank", name="h_ps")
+        def open_bias(n):
+            h_ps = psum.tile([P, FEAT], F32, tag="bank", name="hold_ps")
             h_banks[n] = h_ps
             nc.tensor.matmul(h_ps[:], lhsT=ones_bf[:], rhs=bias_rows[:], start=True, stop=False)
+
+        def linear_c(n):
             for kb in range(K_BLOCKS):
                 nc.tensor.matmul(
-                    h_ps[:],
+                    h_banks[n][:],
                     lhsT=hT_sb[:, n, kb, :],
                     rhs=w_sb[:, kb, :],
                     start=False,
@@ -251,82 +251,80 @@ def tile_gcnlayer_pb_kernel(tc, h_ln, adj, W2, b2, out):
             make_identity(nc, ident_f32[:])
             make_identity(nc, ident_bf[:])
             nc.vector.memset(one[:], 1.0)
-            nc.scalar.sqrt(out=warm[:], in_=one[:])
+            nc.scalar.activation(out=warm[:], in_=one[:], func=ACT.Abs_reciprocal_sqrt)
             nc.vector.memset(hs_codes[:, :, FEAT:MX_COLS].bitcast(I32), 0)
             nc.vector.memset(hs_scales[:, :, FEAT:MX_COLS].bitcast(I32), 0)
 
         with tc.manual_schedule():
             nc.gpsimd.memset(bias_rows[:], 0.0)
             nc.gpsimd.memset(ones_bf[:], 1.0)
+            load_h(0)
             load_adj(0,2)
             nc.sync.dma_start(out=bias_rows[0:1, :], in_=b2.unsqueeze(0))
-            load_h(0)
-            load_adj(2,2)
             nc.sync.dma_start(out=w_sb[:], in_=W2.rearrange("(kb p) f -> p kb f", p=P))
-            load_adj(4,2)
+            load_adj(2,2)
             load_h(4)
+            load_adj(4,2)
             load_adj(6,2)
             consts()
-
-            sum_v(0)
-            sum_v(1)
-            adj_T(0)
-            adj_T(1)
             tr_h(0)
             tr_h(2)
             spread_bias()
-            sum_v(2)
-            q_adj(0,2)
-            sum_v(3)
-            adj_T(2)
-            adj_T(3)
-            dinv_of(0)
+            sum_v(0)
+            adj_T(0)
+            adj_T(1)
+            sum_v(1)
             linear(0)
             bias(0)
+            sum_s(2)
             linear(1)
             bias(1)
-            q_adj(2,2)
+            q_adj(0,2)
             linear(2)
             bias(2)
+            sum_s(3)
             linear(3)
+            dinv_of(0)
             bias(3)
-            recip(0)
-            hs(0,0)
-            hs(0,1)
-            sum_v(6)
-            sum_v(7)
-            q_hs(0,0)
-            q_hs(0,1)
-            sum_s(4)
-            sum_s(5)
             tr_h(4)
             tr_h(6)
-            sq(0)
+            hs(0,0)
+            hs(0,1)
+            adj_T(2)
+            sum_v(4)
             for n in range(4,8):
-                linear_b(n)
-            self_s(0)
+                open_bias(n)
+            for n in range(4,8):
+                linear_c(n)
+            sum_s(5)
             exit_h(4)
-            self_s(1)
+            sum_v(6)
+            sum_v(7)
             exit_h(5)
-            self_s(2)
+            sq(0)
             exit_h(6)
             dinv_of(1)
-            self_s(3)
             exit_h(7)
-            for n in range(4,8):
-                adj_T(n)
-            recip(1)
+            q_hs(0,0)
+            q_hs(0,1)
+            for n in range(3,8):
+                tr_adj(n)
+            for n in range(2):
+                mx(n,0)
+            for n in range(3,8):
+                exit_adj(n)
             hs(1,0)
             hs(1,1)
+            sq(1)
+            for n in range(8):
+                self_s(n)
+            q_adj(2,2)
             q_hs(1,0)
             q_hs(1,1)
             q_adj(4,2)
-            q_adj(6,2)
-            sq(1)
-            for n in range(4,8):
-                self_s(n)
-            for n in range(4):
+            for n in range(2,4):
                 mx(n,0)
+            q_adj(6,2)
             for n in range(4):
                 mx(n,1)
                 finish(n)

@@ -183,9 +183,6 @@ def tile_gcnlayer_pb_kernel(tc, h_ln, adj, W2, b2, out):
                     stop=(kb == K_BLOCKS - 1),
                 )
 
-        def exit_h(n):
-            nc.scalar.copy(out=hb[:, n, :], in_=h_banks[n][:])
-
         def bias(n):
             nc.vector.tensor_tensor(out=hb[:, n, :], in0=h_banks[n][:], in1=bias_sb[:], op=ALU.add)
 
@@ -208,6 +205,23 @@ def tile_gcnlayer_pb_kernel(tc, h_ln, adj, W2, b2, out):
                 out=hs_codes[:, g, f0 : f0 + width].bitcast(FP8X4),
                 scales=hs_scales[:, g, f0 : f0 + width],
                 in_=hs_grouped[:, g, f0 : f0 + width, :].rearrange("p f t -> p (f t)"),
+            )
+
+        def exit_hs(n):
+            nc.scalar.activation(
+                out=hb[:, n, :], in_=h_banks[n][:], func=ACT.Copy, scale=dinv[:, n : n + 1]
+            )
+
+        def group_hs(part):
+            f0, width = FEAT_PARTS[part]
+            nc.vector.tensor_copy(
+                out=hs_grouped[:, 1, f0 : f0 + width, :].rearrange("p (c i) t -> p c t i", i=RUN),
+                in_=hb[:, PACK : 2 * PACK, f0 : f0 + width].rearrange("p t (c i) -> p c t i", i=RUN),
+            )
+
+        def self_1(n):
+            nc.scalar.activation(
+                out=hs_self[:, n, :], in_=hb[:, n, :], func=ACT.Copy, scale=dinv[:, n : n + 1]
             )
 
         def sq(g):
@@ -288,23 +302,24 @@ def tile_gcnlayer_pb_kernel(tc, h_ln, adj, W2, b2, out):
             bias(3)
             tr_h(4)
             tr_h(6)
+            sum_v(4)
+            sum_s(5)
+            sum_v(6)
+            sum_v(7)
+            dinv_of(1)
             hs(0,0)
             hs(0,1)
-            adj_T(2)
-            sum_v(4)
+            tr_adj(2)
             for n in range(4,8):
                 open_bias(n)
             for n in range(4,8):
                 linear_c(n)
-            sum_s(5)
-            exit_h(4)
-            sum_v(6)
-            sum_v(7)
-            exit_h(5)
+            exit_hs(4)
+            exit_adj(2)
+            exit_hs(5)
             sq(0)
-            exit_h(6)
-            dinv_of(1)
-            exit_h(7)
+            exit_hs(6)
+            exit_hs(7)
             q_hs(0,0)
             q_hs(0,1)
             for n in range(3,8):
@@ -313,11 +328,12 @@ def tile_gcnlayer_pb_kernel(tc, h_ln, adj, W2, b2, out):
                 mx(n,0)
             for n in range(3,8):
                 exit_adj(n)
-            hs(1,0)
-            hs(1,1)
-            sq(1)
-            for n in range(8):
+            group_hs(0)
+            group_hs(1)
+            for n in range(4):
                 self_s(n)
+            for n in range(4,8):
+                self_1(n)
             q_adj(2,2)
             q_hs(1,0)
             q_hs(1,1)

@@ -212,6 +212,15 @@ def tile_gcnlayer_pb_kernel(tc, h_ln, adj, W2, b2, out):
                 out=hb[:, n, :], in_=h_banks[n][:], func=ACT.Copy, scale=dinv[:, n : n + 1]
             )
 
+        def exit_hs_v(n):
+            nc.vector.tensor_scalar(
+                out=hb[:, n, :],
+                in0=h_banks[n][:],
+                scalar1=dinv[:, n : n + 1],
+                scalar2=None,
+                op0=ALU.mult,
+            )
+
         def group_hs(part):
             f0, width = FEAT_PARTS[part]
             nc.vector.tensor_copy(
@@ -319,9 +328,9 @@ def tile_gcnlayer_pb_kernel(tc, h_ln, adj, W2, b2, out):
             exit_hs(5)
             sq(0)
             exit_hs(6)
-            exit_hs(7)
             q_hs(0,0)
             q_hs(0,1)
+            exit_hs_v(7)
             for n in range(3,8):
                 tr_adj(n)
             for n in range(2):

import concourse.mybir as mybir
from concourse.masks import make_identity

F32 = mybir.dt.float32
BF16 = mybir.dt.bfloat16
I32 = mybir.dt.int32
U32 = mybir.dt.uint32
U8 = mybir.dt.uint8
FP8X4 = mybir.dt.float8_e4m3fn_x4
ALU = mybir.AluOpType
ACT = mybir.ActivationFunctionType

P = 128
NODES = 1024
FEAT = 384
K_BLOCKS = FEAT // P
PACK = 4
PASSES = NODES // (P * PACK)
TILES = PASSES * PACK
PAIR = 2
HALVES = PACK // PAIR
FEAT_PARTS = ((0, 256), (256, 128))
MX_COLS = 512
RUN = 4
BANKS = 8

FLOPS = 2 * NODES * FEAT * FEAT + 2 * NODES * NODES * FEAT


def tile_gcnlayer_pb_kernel(tc, h_ln, adj, W2, b2, out):
    nc = tc.nc

    h_rows = h_ln.rearrange("(g p t) k -> p g t k", p=P, t=PACK)
    adj_rows = adj.rearrange("(g p t) j -> p g t j", p=P, t=PACK)
    out_rows = out.rearrange("(g p t) f -> p g t f", p=P, t=PACK)

    with (
        tc.tile_pool(name="keep", bufs=1) as keep,
        tc.psum_pool(name="psum", bufs=BANKS) as psum,
    ):
        h_sb = keep.tile([P, TILES, FEAT], BF16)
        w_sb = keep.tile([P, K_BLOCKS, FEAT], BF16)
        adj_sb = keep.tile([P, TILES, NODES], BF16)
        bias_rows = keep.tile([P, FEAT], BF16)
        ones_bf = keep.tile([P, P], BF16)
        bias_sb = keep.tile([P, FEAT], F32)
        ident_bf = keep.tile([P, P], BF16)
        ident_f32 = keep.tile([P, P], F32)
        one = keep.tile([P, 1], F32)
        warm = keep.tile([P, 1], F32)
        hT_sb = keep.tile([P, TILES, K_BLOCKS, P], BF16)
        hb = keep.tile([P, TILES, FEAT], F32)
        hs_self = keep.tile([P, TILES, FEAT], F32)
        row_sums = keep.tile([P, PASSES, 8], F32)
        sum_scratch = keep.tile([P, TILES, NODES], BF16)
        dinv = keep.tile([P, TILES], F32)
        dinv_sq = keep.tile([P, TILES], F32)
        adj_grouped = keep.tile([P, TILES, PASSES, P, PACK], BF16, align_bytes=64)
        adj_codes = keep.tile([P, TILES, PASSES, P], U32, align_bytes=64)
        adj_scales = keep.tile([P, TILES, PASSES, P], U8, align_bytes=64)
        hs_grouped = keep.tile([P, PASSES, FEAT, PACK], BF16, align_bytes=64)
        hs_codes = keep.tile([P, PASSES, MX_COLS], U32, align_bytes=64)
        hs_scales = keep.tile([P, PASSES, MX_COLS], U8, align_bytes=64)
        out_sb = keep.tile([P, TILES, FEAT], F32)

        adj_words = adj_sb[:].bitcast(F32)

        adj_grouped_words = adj_grouped[:].bitcast(F32)

        agg_banks = {}

        def load_adj(n, count=1):
            g, t = divmod(n, PACK)
            nc.sync.dma_start(out=adj_sb[:, n : n + count, :], in_=adj_rows[:, g, t : t + count, :])

        def load_h(n, count=PACK):
            g, t = divmod(n, PACK)
            nc.sync.dma_start(out=h_sb[:, n : n + count, :], in_=h_rows[:, g, t : t + count, :])

        def spread_bias():
            bias_ps = psum.tile([P, FEAT], F32, tag="bank")
            nc.tensor.matmul(bias_ps[:], lhsT=ones_bf[:], rhs=bias_rows[:], start=True, stop=True)
            nc.scalar.copy(out=bias_sb[:], in_=bias_ps[:])

        def sum_v(n):
            g, t = divmod(n, PACK)
            nc.vector.scalar_tensor_tensor(
                out=sum_scratch[:, n, :].bitcast(F32),
                in0=adj_sb[:, n, 0 : NODES // 2],
                scalar=1.0,
                in1=adj_sb[:, n, NODES // 2 : NODES],
                op0=ALU.mult,
                op1=ALU.add,
                accum_out=row_sums[:, g, t : t + 1],
            )

        def sum_s(n):
            g, t = divmod(n, PACK)
            nc.scalar.activation(
                out=sum_scratch[:, n, :],
                in_=adj_sb[:, n, :],
                func=ACT.Copy,
                accum_out=row_sums[:, g, t : t + 1],
            )

        def dinv_of(g):
            four = slice(g * PACK, (g + 1) * PACK)
            nc.scalar.activation(
                out=dinv[:, four],
                in_=row_sums[:, g, 0:PACK],
                func=ACT.Abs_reciprocal_sqrt,
                bias=1.0,
            )

        adjT = {}

        def tr_adj(n):
            adjT_ps = psum.tile([P, PASSES * HALVES, P], F32, tag="bank", name="adjT_ps")
            adjT[n] = adjT_ps
            for b in range(PASSES * HALVES):
                g, u = divmod(b, HALVES)
                first = g * P * HALVES + u
                nc.tensor.transpose(
                    adjT_ps[:, b, :],
                    adj_words[:, n, first : (g + 1) * P * HALVES : HALVES],
                    ident_f32[:],
                )

        def exit_adj(n, on_vector=False):
            src = adjT[n][:].rearrange("p (g u) i -> p g i u", u=HALVES)
            if on_vector:
                nc.vector.tensor_copy(out=adj_grouped_words[:, n], in_=src)
            else:
                nc.scalar.copy(out=adj_grouped_words[:, n], in_=src)

        def adj_T(n):
            tr_adj(n)
            exit_adj(n)

        def q_adj(n, count=1):
            tiles = slice(n, n + count)
            nc.vector.quantize_mx(
                out=adj_codes[:, tiles].rearrange("p n g i -> p (n g i)").bitcast(FP8X4),
                scales=adj_scales[:, tiles].rearrange("p n g i -> p (n g i)"),
                in_=adj_grouped[:, tiles].rearrange("p n g i t -> p (n g i t)"),
            )

        def tr_h(n):
            hT_ps = psum.tile([P, PAIR, K_BLOCKS, P], BF16, tag="bank")
            for e in range(PAIR):
                for kb in range(K_BLOCKS):
                    nc.tensor.transpose(
                        hT_ps[:, e, kb, :], h_sb[:, n + e, kb * P : (kb + 1) * P], ident_bf[:]
                    )
            nc.scalar.copy(out=hT_sb[:, n : n + PAIR], in_=hT_ps[:])

        h_banks = {}

        def linear(n):
            h_ps = psum.tile([P, FEAT], F32, tag="bank", name="h_ps")
            h_banks[n] = h_ps
            for kb in range(K_BLOCKS):
                nc.tensor.matmul(
                    h_ps[:],
                    lhsT=hT_sb[:, n, kb, :],
                    rhs=w_sb[:, kb, :],
                    start=(kb == 0),
                    stop=(kb == K_BLOCKS - 1),
                )

        def open_bias(n):
            h_ps = psum.tile([P, FEAT], F32, tag="bank", name="hold_ps")
            h_banks[n] = h_ps
            nc.tensor.matmul(h_ps[:], lhsT=ones_bf[:], rhs=bias_rows[:], start=True, stop=False)

        def linear_c(n):
            for kb in range(K_BLOCKS):
                nc.tensor.matmul(
                    h_banks[n][:],
                    lhsT=hT_sb[:, n, kb, :],
                    rhs=w_sb[:, kb, :],
                    start=False,
                    stop=(kb == K_BLOCKS - 1),
                )

        def bias(n):
            nc.vector.tensor_tensor(out=hb[:, n, :], in0=h_banks[n][:], in1=bias_sb[:], op=ALU.add)

        def hs(g, part):
            four = slice(g * PACK, (g + 1) * PACK)
            f0, width = FEAT_PARTS[part]
            nc.vector.tensor_tensor(
                out=hs_grouped[:, g, f0 : f0 + width, :].rearrange("p (c i) t -> p c t i", i=RUN),
                in0=hb[:, four, f0 : f0 + width].rearrange("p t (c i) -> p c t i", i=RUN),
                in1=dinv[:, four]
                .unsqueeze(1)
                .unsqueeze(3)
                .to_broadcast([P, width // RUN, PACK, RUN]),
                op=ALU.mult,
            )

        def q_hs(g, part):
            f0, width = FEAT_PARTS[part]
            nc.vector.quantize_mx(
                out=hs_codes[:, g, f0 : f0 + width].bitcast(FP8X4),
                scales=hs_scales[:, g, f0 : f0 + width],
                in_=hs_grouped[:, g, f0 : f0 + width, :].rearrange("p f t -> p (f t)"),
            )

        def exit_hs(n):
            nc.scalar.activation(
                out=hb[:, n, :], in_=h_banks[n][:], func=ACT.Copy, scale=dinv[:, n : n + 1]
            )

        def exit_hs_v(n):
            nc.vector.tensor_scalar(
                out=hb[:, n, :],
                in0=h_banks[n][:],
                scalar1=dinv[:, n : n + 1],
                scalar2=None,
                op0=ALU.mult,
            )

        def group_hs(part):
            f0, width = FEAT_PARTS[part]
            nc.vector.tensor_copy(
                out=hs_grouped[:, 1, f0 : f0 + width, :].rearrange("p (c i) t -> p c t i", i=RUN),
                in_=hb[:, PACK : 2 * PACK, f0 : f0 + width].rearrange("p t (c i) -> p c t i", i=RUN),
            )

        def self_1(n):
            nc.scalar.activation(
                out=hs_self[:, n, :], in_=hb[:, n, :], func=ACT.Copy, scale=dinv[:, n : n + 1]
            )

        def sq(g):
            four = slice(g * PACK, (g + 1) * PACK)
            nc.scalar.square(out=dinv_sq[:, four], in_=dinv[:, four])

        def self_s(n):
            nc.scalar.activation(
                out=hs_self[:, n, :], in_=hb[:, n, :], func=ACT.Copy, scale=dinv_sq[:, n : n + 1]
            )

        def mx(n, g, first=None, last=None):
            if n not in agg_banks:
                agg_banks[n] = psum.tile([P, MX_COLS], F32, tag="bank", name="agg_ps")
            nc.tensor.matmul_mx(
                out=agg_banks[n][:],
                lhsT=adj_codes[:, n, g, :].bitcast(FP8X4),
                lhsT_scale=adj_scales[:, n, g, :],
                rhs=hs_codes[:, g, :].bitcast(FP8X4),
                rhs_scale=hs_scales[:, g, :],
                start=(g == 0),
                stop=(g == PASSES - 1),
            )

        def finish(n):
            nc.vector.scalar_tensor_tensor(
                out=out_sb[:, n, :],
                in0=agg_banks[n][:, 0:FEAT],
                scalar=dinv[:, n : n + 1],
                in1=hs_self[:, n, :],
                op0=ALU.mult,
                op1=ALU.add,
            )
            store(n)

        def store(n):
            g, t = divmod(n, PACK)
            nc.sync.dma_start(out=out_rows[:, g, t, :], in_=out_sb[:, n, :])

        def consts():
            make_identity(nc, ident_f32[:])
            make_identity(nc, ident_bf[:])
            nc.vector.memset(one[:], 1.0)
            nc.scalar.activation(out=warm[:], in_=one[:], func=ACT.Abs_reciprocal_sqrt)
            nc.vector.memset(hs_codes[:, :, FEAT:MX_COLS].bitcast(I32), 0)
            nc.vector.memset(hs_scales[:, :, FEAT:MX_COLS].bitcast(I32), 0)

        with tc.manual_schedule():
            nc.gpsimd.memset(bias_rows[:], 0.0)
            nc.gpsimd.memset(ones_bf[:], 1.0)
            load_h(0)
            load_adj(0,2)
            nc.sync.dma_start(out=bias_rows[0:1, :], in_=b2.unsqueeze(0))
            nc.sync.dma_start(out=w_sb[:], in_=W2.rearrange("(kb p) f -> p kb f", p=P))
            load_adj(2,2)
            load_h(4)
            load_adj(4,2)
            load_adj(6,2)
            consts()
            tr_h(0)
            tr_h(2)
            spread_bias()
            sum_v(0)
            adj_T(0)
            adj_T(1)
            sum_v(1)
            linear(0)
            bias(0)
            sum_s(2)
            linear(1)
            bias(1)
            q_adj(0,2)
            linear(2)
            bias(2)
            sum_s(3)
            linear(3)
            dinv_of(0)
            bias(3)
            tr_h(4)
            tr_h(6)
            sum_v(4)
            sum_s(5)
            sum_v(6)
            sum_v(7)
            dinv_of(1)
            hs(0,0)
            hs(0,1)
            tr_adj(2)
            for n in range(4,8):
                open_bias(n)
            for n in range(4,8):
                linear_c(n)
            exit_hs(4)
            exit_adj(2)
            exit_hs(5)
            sq(0)
            exit_hs(6)
            q_hs(0,0)
            q_hs(0,1)
            exit_hs_v(7)
            for n in range(3,8):
                tr_adj(n)
            for n in range(2):
                mx(n,0)
            for n in range(3,8):
                exit_adj(n)
            group_hs(0)
            group_hs(1)
            for n in range(4):
                self_s(n)
            for n in range(4,8):
                self_1(n)
            q_adj(2,2)
            q_hs(1,0)
            q_hs(1,1)
            q_adj(4,2)
            for n in range(2,4):
                mx(n,0)
            q_adj(6,2)
            for n in range(4):
                mx(n,1)
                finish(n)
            for n in range(4,8):
                mx(n,0)
                mx(n,1)
                finish(n)
